import numpy as np
import ml_dtypes


def mxq(x, axis, fmt="e4m3"):
    dtype, down = {"e4m3": (ml_dtypes.float8_e4m3fn, 7), "e5m2": (ml_dtypes.float8_e5m2, 14)}[fmt]
    v = np.moveaxis(np.asarray(x, np.float32).astype(ml_dtypes.bfloat16).astype(np.float64), axis, -1)
    blocks = v.reshape(v.shape[:-1] + (-1, 32))
    amax = np.abs(blocks).max(-1, keepdims=True)
    byte = np.maximum(np.where(amax > 0, np.frexp(amax)[1] - 1 + 127, 0) - down, 1)
    scale = np.exp2(byte - 127.0)
    codes = (blocks / scale).astype(np.float32).astype(dtype).astype(np.float64)
    return np.moveaxis((codes * scale).reshape(v.shape), -1, axis)


WIDE = False


def mx_kscale(k):
    if not WIDE:
        return np.ones(k)
    levels = np.array([18, -18])
    if k % 512:
        return np.exp2(np.random.permutation(np.resize(levels, k // 32))).repeat(32)
    a = np.empty((k // 512, 16))
    for p in range(k // 512):
        a[p, :8] = np.random.permutation(np.resize(levels, 8))
        for g in range(8):
            far = levels[np.abs(levels - a[p, g]) >= 10]
            a[p, g + 8] = far[np.random.randint(len(far))]
    return np.exp2(a.ravel()).repeat(32)


BF16 = ml_dtypes.bfloat16


def bf(x):
    return np.asarray(x, np.float32).astype(BF16)


def f64(x):
    return np.asarray(x).astype(np.float64)


B, NV, S, D, H = 2, 6, 128, 1024, 8
HD = D // H
T = B * NV * S


def setup_inputs():
    st = mx_kscale(T)
    s = np.repeat(st[::32][::5][:B * S // 32], 32).reshape(B, 1, S)
    s = np.repeat(s, NV, axis=1).reshape(B * NV, S, 1)
    u = mx_kscale(D)
    v = mx_kscale(D)
    x0 = bf(np.random.standard_normal((B * NV, S, D)))
    scores = bf(np.random.standard_normal((B, NV, NV, H, S)) * 1.4)
    Wv0 = bf(np.random.standard_normal((D, D)) / np.sqrt(D))
    bv = bf(np.random.standard_normal(D) * 0.3)
    Wo0 = bf(np.random.standard_normal((D, D)) / np.sqrt(D))
    bo = bf(np.random.standard_normal(D) * 0.3)
    g = bf(np.random.standard_normal((B * NV, S, D)) * np.exp2(np.random.randint(-6, 1, (B * NV, S, 1))) / s * u)
    sc = f64(scores)
    e = np.exp(sc - sc.max(2, keepdims=True))
    w = e / e.sum(2, keepdims=True)
    return {"x": bf(f64(x0) * s),
            "scores": scores,
            "Wv": bf(f64(Wv0) / v),
            "bv": bv,
            "Wo": bf(f64(Wo0) * v[:, None] / u),
            "bo": bo,
            "w": np.asarray(w, np.float32),
            "grad_out": g}


def reference(x, scores, Wv, bv, Wo, bo, w, grad_out):
    g = f64(grad_out).reshape(T, D)
    dm = mxq(g, 1, "e5m2") @ mxq(f64(Wo), 1, "e4m3").T
    dm = dm.reshape(B, NV, S, H, HD)
    wf = f64(w)
    dv = np.zeros((B, NV, S, H, HD))
    for i in range(NV):
        dv = dv + wf[:, i].transpose(0, 1, 3, 2)[..., None] * dm[:, i][:, None]
    dv = dv.reshape(T, D)
    dx = mxq(dv, 1, "e5m2") @ mxq(f64(Wv), 1, "e4m3").T
    dWv = mxq(f64(x).reshape(T, D), 0, "e4m3").T @ mxq(dv, 0, "e5m2")
    return dx.reshape(B * NV, S, D), dWv

@@ -1,0 +1,527 @@
+from contextlib import ExitStack
+
+import concourse.mybir as mybir
+from concourse.masks import make_identity
+
+F32 = mybir.dt.float32
+BF16 = mybir.dt.bfloat16
+U32 = mybir.dt.uint32
+U8 = mybir.dt.uint8
+E4M3 = mybir.dt.float8_e4m3fn_x4
+E5M2 = mybir.dt.float8_e5m2_x4
+ALU = mybir.AluOpType
+AXIS = mybir.AxisListType
+
+SCENES, VIEWS, S, D, HEADS = 2, 6, 128, 1024, 8
+TOKENS = SCENES * VIEWS * S
+P = 128
+BANK = 512
+POS = 20
+CHUNKS = 3
+ROWS = VIEWS * POS
+REST = 4
+GROUP = CHUNKS * POS + REST
+REST_TILE = 4 * CHUNKS
+JH = VIEWS * HEADS
+PARK_ROW = 256
+
+FLOPS = 3 * 2 * TOKENS * D * D + 2 * VIEWS * TOKENS * D
+BYTES = 2 * (2 * TOKENS * D + 2 * D * D) + 4 * SCENES * VIEWS * VIEWS * HEADS * S + 4 * (TOKENS * D + D * D)
+
+
+def weave(jobs, side):
+    done = 0
+    for n, job in enumerate(jobs):
+        job()
+        upto = (n + 1) * len(side) // len(jobs)
+        for step in side[done:upto]:
+            step()
+        done = upto
+
+
+def runs(first, second, a, b):
+    merged = []
+    for n in range(max(-(-len(first) // a), -(-len(second) // b))):
+        merged.extend(first[n * a : (n + 1) * a])
+        merged.extend(second[n * b : (n + 1) * b])
+    return merged
+
+
+def tile_crossviewattention_pa_v_kernel(tc, x, scores, Wv, bv, Wo, bo, w, grad_out, out_0, out_1):
+    nc = tc.nc
+    with ExitStack() as ctx:
+        sb = ctx.enter_context(tc.tile_pool(name="sb", bufs=1))
+        psum = ctx.enter_context(tc.psum_pool(name="psum", bufs=8))
+        ctx.enter_context(tc.manual_schedule())
+
+        def tile(name, shape, dtype, tag=None, bufs=1):
+            return sb.tile(shape, dtype, name=name, tag=tag or name, bufs=bufs, align_bytes=64)
+
+        def bank():
+            return psum.tile([P, BANK], F32, name="bank", tag="bank")
+
+        def act(out, in_):
+            nc.scalar.copy(out=out, in_=in_)
+
+        def dve(out, in_):
+            nc.vector.tensor_copy(out=out, in_=in_)
+
+        def quantize(codes, scales, values, fmt):
+            nc.vector.quantize_mx(out=codes.bitcast(fmt), scales=scales, in_=values)
+
+        raw = {}
+
+        def load_rows(key, src):
+            t = tile("raw", [P, 2, D], BF16, bufs=8)
+            nc.sync.dma_start(out=t[:], in_=src)
+            raw[key] = t
+
+        def load_weight(name, W, r):
+            load_rows((name, r), W[2 * P * r : 2 * P * (r + 1), :].rearrange("(a p) k -> p a k", p=P))
+
+        def load_g(r):
+            load_rows(("g", r), grad_out[2 * r : 2 * r + 2].rearrange("v s k -> s v k"))
+
+        x_rows = x.rearrange("v s d -> (v s) d")
+
+        def load_x(n):
+            gam, half = divmod(n, 2)
+            t = tile("raw", [P, 4, BANK], BF16, bufs=8)
+            src = x_rows[512 * gam : 512 * (gam + 1), BANK * half : BANK * (half + 1)]
+            nc.sync.dma_start(out=t[:], in_=src.rearrange("(p j) d -> p j d", j=4))
+            raw["x", n] = t
+
+        w_in = tile("w_in", [P, VIEWS, S], F32, tag="back", bufs=2)
+
+        def load_w():
+            for b in range(SCENES):
+                nc.sync.dma_start(out=w_in[JH * b : JH * (b + 1)], in_=w[b].rearrange("i j h s -> (j h) i s"))
+
+        for r in range(2):
+            load_weight("wo", Wo, r)
+        for r in range(3):
+            load_g(r)
+        for r in range(2, 4):
+            load_weight("wo", Wo, r)
+        load_g(3)
+
+        ident = tile("ident", [P, P], F32)
+        make_identity(nc, ident[:])
+        w_sorted = tile("w_sorted", [P, 7, P], F32, tag="back", bufs=2)
+        nc.vector.memset(w_sorted[:], 0.0)
+        g_stage = [tile("g_stage", [P, 6, 2, P, 2], F32, tag="wide", bufs=2) for b in range(SCENES)]
+        g_rest = tile("g_rest", [P, 2, P, 2], F32)
+        for b in range(SCENES):
+            nc.vector.memset(g_stage[b][:, :, :, ROWS:, :], 0.0)
+        nc.vector.memset(g_rest[:, :, 2 * JH :, :], 0.0)
+        perm = tile("perm", [P, P], F32)
+        dve(perm[:, :ROWS].rearrange("r (u p e) -> r u p e", u=2, e=2), ident[:, :ROWS].rearrange("r (p u e) -> r u p e", u=2, e=2))
+        dve(perm[:, ROWS:].rearrange("r (u p e) -> r u p e", u=2, e=2), ident[:, ROWS:].rearrange("r (p u e) -> r u p e", u=2, e=2))
+        mask = tile("mask", [P, POS], F32)
+        nc.vector.tensor_reduce(out=mask[:], in_=ident[:, :ROWS].rearrange("r (i s) -> r s i", i=VIEWS), axis=AXIS.X, op=ALU.add)
+        mask_rest = tile("mask_rest", [P, SCENES, 8], F32)
+        nc.vector.tensor_reduce(
+            out=mask_rest[:], in_=ident[:, : 2 * JH].rearrange("r (b i s) -> r b s i", b=SCENES, i=VIEWS), axis=AXIS.X, op=ALU.add
+        )
+
+        used = 2 * JH
+
+        def sort_w():
+            for u in range(2):
+                dve(
+                    w_sorted[:used, CHUNKS * u : CHUNKS * (u + 1), :ROWS].rearrange("q k (i p e) -> q k i p e", i=VIEWS, e=2),
+                    w_in[:used, :, :ROWS].rearrange("q i (k p u e) -> q u k i p e", k=CHUNKS, u=2, e=2)[:, u],
+                )
+            for b in range(SCENES):
+                dve(
+                    w_sorted[:used, 6, JH * b : JH * (b + 1)].rearrange("q (i u p e) -> q i u p e", i=VIEWS, u=2, e=2),
+                    w_in[:used, :, ROWS:].rearrange("q i (p u e) -> q i u p e", u=2, e=2),
+                )
+
+        w_rows = tile("w_rows", [P, SCENES, 6, HEADS, VIEWS], F32)
+        w_rows_rest = tile("w_rows_rest", [P, SCENES, HEADS, VIEWS], F32)
+
+        def turn_w(first, count):
+            acc = bank()
+            slots = acc[:].rearrange("r (n c) -> r n c", c=P)
+            for n in range(count):
+                nc.tensor.transpose(slots[:, n, :], w_sorted[:, first + n, :], ident[:])
+            main = min(count, 6 - first)
+            act(
+                w_rows[:, :, first : first + main].rearrange("r b n h j -> r n b h j"),
+                slots[:, :main, :used].rearrange("r n (b j h) -> r n b h j", b=SCENES, j=VIEWS),
+            )
+            if main < count:
+                act(w_rows_rest[:], slots[:, main, :used].rearrange("r (b j h) -> r b h j", b=SCENES, j=VIEWS))
+
+        mix_w = {}
+
+        def build_w(st, lo, hi):
+            b, u = divmod(st, 2)
+            if lo == 0:
+                mix_w[st] = tile("mix_w", [P, POS, CHUNKS * JH], F32, bufs=2)
+            src = w_rows[:, b, CHUNKS * u : CHUNKS * (u + 1)].rearrange("r k h j -> r (k h j)")
+            for s in range(lo, hi):
+                nc.vector.tensor_scalar(out=mix_w[st][:, s, :], in0=src, scalar1=mask[:, s : s + 1], scalar2=None, op0=ALU.mult)
+
+        def build_steps(st):
+            return [lambda lo=lo: build_w(st, lo, lo + 5) for lo in range(0, POS, 5)]
+
+        mix_w_rest = tile("mix_w_rest", [P, SCENES, 8, JH], F32)
+
+        def build_w_rest(b):
+            src = w_rows_rest[:, b].rearrange("r h j -> r (h j)")
+            for s in range(8):
+                nc.vector.tensor_scalar(
+                    out=mix_w_rest[:, b, s, :], in0=src, scalar1=mask_rest[:, b, s : s + 1], scalar2=None, op0=ALU.mult
+                )
+
+        w_codes = {name: tile(name + "_codes", [P, 2, D], U32) for name in ("wo", "wv")}
+        w_scales = {name: tile(name + "_scales", [P, 2, D], U8) for name in ("wo", "wv")}
+        stage = {}
+
+        def new_stage(key, width=BANK):
+            stage[key] = tile("stage", [P, width, 4], BF16, bufs=4)
+
+        def stage_words(key):
+            return stage[key][:].rearrange("p c t -> p (c t)").bitcast(F32)
+
+        ordered = {}
+
+        def sort_words(key):
+            ordered[key] = tile("ordered", [P, 4, 2, P], F32, bufs=3)
+            words = raw[key][:].rearrange("p a k -> p (a k)").bitcast(F32)
+            dve(ordered[key][:], words.rearrange("p (n c u) -> p n u c", n=4, u=2))
+
+        def half_words(key, a, g, u):
+            if key in ordered:
+                return ordered[key][:, 2 * a + g, u, :]
+            return raw[key][:, a, :].bitcast(F32)[:, 256 * g + u : 256 * (g + 1) : 2]
+
+        def turn_weight(name, r, g, copy):
+            half, part = divmod(r, 2)
+            if part == 0:
+                new_stage((name, half, g))
+            acc = bank()
+            slots = acc[:].rearrange("p (a u c) -> p a u c", a=2, u=2)
+            for a in range(2):
+                for u in range(2):
+                    nc.tensor.transpose(slots[:, a, u, :], half_words((name, r), a, g, u), ident[:])
+            dst = stage_words((name, half, g))[:, BANK * part : BANK * (part + 1)]
+            copy(dst.rearrange("p (a c u) -> p a c u", a=2, u=2), slots.rearrange("p a u c -> p a c u"))
+
+        def quantize_weight(name, half, g):
+            cols = slice(BANK * half, BANK * (half + 1))
+            values = stage[name, half, g][:].rearrange("p c t -> p (c t)")
+            quantize(w_codes[name][:, g, cols], w_scales[name][:, g, cols], values, E4M3)
+
+        g_codes = tile("g_codes", [P, REST_TILE + 1, 2 * P], U32, tag="codes")
+        g_scales = tile("g_scales", [P, REST_TILE + 1, 2 * P], U8, tag="scales")
+
+        def turn_g(v, copy):
+            b, i = divmod(v, VIEWS)
+            acc = bank()
+            slots = acc[:].rearrange("p (g u n) -> p g u n", g=2, u=2)
+            for g in range(2):
+                for u in range(2):
+                    nc.tensor.transpose(slots[:, g, u, :], half_words(("g", v // 2), v % 2, g, u), perm[:])
+            copy(
+                g_stage[b][:, :, :, POS * i : POS * (i + 1), :].rearrange("p k g s u -> p g k s u"),
+                slots[:, :, :, :ROWS].rearrange("p g u (k s) -> p g k s u", s=POS),
+            )
+            col = JH * b + 8 * i
+            copy(g_rest[:, :, col : col + 8, :], slots[:, :, :, ROWS:].rearrange("p g u s -> p g s u"))
+
+        def quantize_g(n):
+            src = g_rest[:] if n == REST_TILE else g_stage[n // 6][:, n % 6]
+            values = src.rearrange("p g c u -> p (g c u)").bitcast(BF16)
+            quantize(g_codes[:, n, :], g_scales[:, n, :], values, E5M2)
+
+        dm = {}
+
+        def dmixed(n, half, copy):
+            if half == 0:
+                if n == REST_TILE:
+                    dm[n] = tile("dm_rest", [P, D], F32)
+                else:
+                    dm[n] = tile("dm", [P, D], F32, bufs=6)
+            cols = slice(BANK * half, BANK * (half + 1))
+            acc = bank()
+            for g in range(2):
+                rows = slice(P * g, P * (g + 1))
+                nc.tensor.matmul_mx(
+                    out=acc[:],
+                    lhsT=g_codes[:, n, rows].bitcast(E5M2),
+                    lhsT_scale=g_scales[:, n, rows],
+                    rhs=w_codes["wo"][:, g, cols].bitcast(E4M3),
+                    rhs_scale=w_scales["wo"][:, g, cols],
+                    start=(g == 0),
+                    stop=(g == 1),
+                )
+            copy(dm[n][:, cols], acc[:])
+
+        dv_t = {(u, g): tile("dv_t%d%d" % (u, g), [P, 4, SCENES * VIEWS, GROUP], BF16) for u in range(2) for g in range(2)}
+
+        def mix(st, h, copy):
+            b, u = divmod(st, 2)
+            acc = bank()
+            for k in range(CHUNKS):
+                col = JH * k + VIEWS * h
+                nc.tensor.matmul(
+                    out=acc[:, ROWS * k : ROWS * (k + 1)].rearrange("c (s j) -> c s j", j=VIEWS),
+                    lhsT=dm[CHUNKS * st + k][:, P * h : P * (h + 1)],
+                    rhs=mix_w[st][:, :, col : col + VIEWS],
+                    start=True,
+                    stop=True,
+                )
+            copy(
+                dv_t[u, h // 4][:, h % 4, VIEWS * b : VIEWS * (b + 1), : CHUNKS * POS],
+                acc[:, : CHUNKS * ROWS].rearrange("c (q j) -> c j q", j=VIEWS),
+            )
+
+        def mix_rest(g, copy):
+            acc = bank()
+            for hq in range(4):
+                h = 4 * g + hq
+                nc.tensor.matmul(
+                    out=acc[:, used * hq : used * (hq + 1)].rearrange("c (s j) -> c s j", j=VIEWS),
+                    lhsT=dm[REST_TILE][:, P * h : P * (h + 1)],
+                    rhs=mix_w_rest[:].rearrange("r b s m -> r (b s) m")[:, :, VIEWS * h : VIEWS * (h + 1)],
+                    start=True,
+                    stop=True,
+                )
+            src = acc[:, : 4 * used].rearrange("c (h b u q j) -> c u h b j q", h=4, b=SCENES, u=2, j=VIEWS)
+            for u in range(2):
+                dst = dv_t[u, g][:, :, :, CHUNKS * POS :].rearrange("c h (b j) q -> c h b j q", b=SCENES)
+                copy(dst, src[:, u])
+
+        width = VIEWS * GROUP
+        back = {}
+        f_codes, f_scales = {}, {}
+
+        def parking(st, g):
+            rows = out_1[PARK_ROW + 192 * st : PARK_ROW + 192 * (st + 1), :]
+            return rows.bitcast(BF16).rearrange("a b -> (a b)").rearrange("(c m) -> c m", m=width)[BANK * g : BANK * (g + 1), :]
+
+        def park(st, g):
+            b, u = divmod(st, 2)
+            src = dv_t[u, g][:, :, VIEWS * b : VIEWS * (b + 1), :].rearrange("c h v q -> c h (v q)")
+            nc.sync.dma_start(out=parking(st, g).rearrange("(h c) m -> c h m", c=P), in_=src)
+
+        def fetch(st, g):
+            back[st, g] = tile("back", [P, 4, width], BF16, tag="back", bufs=2)
+            nc.sync.dma_start(out=back[st, g][:], in_=parking(st, g).rearrange("(p t) m -> p t m", t=4))
+
+        def interleave(key, src):
+            dve(stage[key][:].rearrange("p (c i) t -> p c t i", i=4), src.rearrange("p t (c i) -> p c t i", i=4))
+
+        def weave_dv(st, g):
+            new_stage(("f", st, g), width)
+            interleave(("f", st, g), back[st, g][:])
+
+        def quantize_dv_features(st, g):
+            if g == 0:
+                f_codes[st] = tile("f_codes", [P, 2, width], U32, bufs=2)
+                f_scales[st] = tile("f_scales", [P, 2, width], U8, bufs=2)
+            values = stage["f", st, g][:].rearrange("p c t -> p (c t)")
+            for lo, hi in ((0, 256), (256, width)):
+                quantize(f_codes[st][:, g, lo:hi], f_scales[st][:, g, lo:hi], values[:, 4 * lo : 4 * hi], E5M2)
+
+        x_codes = tile("x_codes", [P, 3, D], U32)
+        x_scales = tile("x_scales", [P, 3, D], U8)
+
+        def weave_x(n):
+            new_stage(("x", n))
+            interleave(("x", n), raw["x", n][:])
+
+        def quantize_x(n):
+            gam, half = divmod(n, 2)
+            cols = slice(BANK * half, BANK * (half + 1))
+            quantize(x_codes[:, gam, cols], x_scales[:, gam, cols], stage["x", n][:].rearrange("p c t -> p (c t)"), E4M3)
+
+        t_planes = {}
+
+        def turn_dv(gam, g, part, copy):
+            if part == 0:
+                new_stage(("t", gam, g))
+            acc = bank()
+            slots = acc[:].rearrange("p (a u c) -> p a u c", a=2, u=2)
+            for a in range(2):
+                for u in range(2):
+                    words = dv_t[u, g][:, 2 * part + a].rearrange("c v q -> c (v q)").bitcast(F32)
+                    nc.tensor.transpose(slots[:, a, u, :], words[:, P * gam : P * (gam + 1)], ident[:])
+            dst = stage_words(("t", gam, g))[:, BANK * part : BANK * (part + 1)]
+            copy(dst.rearrange("p (a c u) -> p a c u", a=2, u=2), slots.rearrange("p a u c -> p a c u"))
+
+        def quantize_dv_tokens(gam, g):
+            if not t_planes:
+                t_planes["codes"] = tile("t_codes", [P, 3, D], U32, tag="codes")
+                t_planes["scales"] = tile("t_scales", [P, 3, D], U8, tag="scales")
+            cols = slice(BANK * g, BANK * (g + 1))
+            values = stage["t", gam, g][:].rearrange("p c t -> p (c t)")
+            quantize(t_planes["codes"][:, gam, cols], t_planes["scales"][:, gam, cols], values, E5M2)
+
+        ring = []
+        taken = []
+
+        def out_slot():
+            if not ring:
+                for n in range(2):
+                    t = tile("ring", [P, 3, D], F32, tag="wide", bufs=2)
+                    ring.extend(t[:, k, :] for k in range(3))
+            taken.append(ring[len(taken) % len(ring)])
+            return taken[-1]
+
+        dx_rows = out_0.rearrange("v (p u e) d -> u e (v p) d", u=2, e=2)
+        held = {}
+
+        def grad_x(st, m, half, copy):
+            b, u = divmod(st, 2)
+            if half == 0:
+                held[st, m] = out_slot()
+            cols = slice(BANK * half, BANK * (half + 1))
+            rows = slice(P * m, P * (m + 1))
+            acc = bank()
+            for g in range(2):
+                nc.tensor.matmul_mx(
+                    out=acc[:],
+                    lhsT=f_codes[st][:, g, rows].bitcast(E5M2),
+                    lhsT_scale=f_scales[st][:, g, rows],
+                    rhs=w_codes["wv"][:, g, cols].bitcast(E4M3),
+                    rhs_scale=w_scales["wv"][:, g, cols],
+                    start=(g == 0),
+                    stop=(g == 1),
+                )
+            copy(held[st, m][:, cols], acc[:])
+            if half == 1:
+                first = 32 * (VIEWS * b + 2 * m)
+                for e in range(2):
+                    nc.sync.dma_start(out=dx_rows[u, e, first : first + 64, :], in_=held[st, m][e::2, :])
+
+        def grad_w(g, m, copy):
+            if m % 2 == 0:
+                held[g, "w", m // 2] = out_slot()
+            dst = held[g, "w", m // 2][:, BANK * (m % 2) : BANK * (m % 2 + 1)]
+            cols = slice(BANK * g, BANK * (g + 1))
+            rows = slice(P * m, P * (m + 1))
+            acc = bank()
+            for gam in range(3):
+                nc.tensor.matmul_mx(
+                    out=acc[:],
+                    lhsT=x_codes[:, gam, rows].bitcast(E4M3),
+                    lhsT_scale=x_scales[:, gam, rows],
+                    rhs=t_planes["codes"][:, gam, cols].bitcast(E5M2),
+                    rhs_scale=t_planes["scales"][:, gam, cols],
+                    start=(gam == 0),
+                    stop=(gam == 2),
+                )
+            copy(dst, acc[:])
+            nc.sync.dma_start(out=out_1[rows, cols], in_=dst)
+
+        def step(fn, *args):
+            return lambda: fn(*args)
+
+        def both(*steps):
+            return lambda: [s() for s in steps]
+
+        turns = (act, dve)
+
+        def dmixed_jobs(st, engines=(act,)):
+            tiles = [(CHUNKS * st + k, half) for half in range(2) for k in range(CHUNKS)]
+            return [step(dmixed, n, half, engines[c % len(engines)]) for c, (n, half) in enumerate(tiles)]
+
+        def mix_jobs(st, engines=(act,)):
+            jobs = [step(mix, st, h, engines[h % len(engines)]) for h in range(HEADS)]
+            for g in range(2):
+                jobs[4 * g + 3] = both(jobs[4 * g + 3], step(park, st, g))
+            return jobs
+
+        def grad_x_jobs(st, engines=(act,)):
+            tiles = [(m, half) for m in range(3) for half in range(2)]
+            return [step(grad_x, st, m, half, engines[c % len(engines)]) for c, (m, half) in enumerate(tiles)]
+
+        def turn_dv_jobs(gam, g, engines=(act,)):
+            return [step(turn_dv, gam, g, part, engines[part % len(engines)]) for part in range(2)]
+
+        def feature_steps(st):
+            return [
+                step(weave_dv, st, 0),
+                step(weave_dv, st, 1),
+                step(quantize_dv_features, st, 0),
+                step(quantize_dv_features, st, 1),
+            ]
+
+        def fetch_steps(st):
+            return [step(fetch, st, 0), step(fetch, st, 1)]
+
+        def x_steps(n):
+            return [step(weave_x, n), step(weave_x, n + 1), step(quantize_x, n), step(quantize_x, n + 1)]
+
+        later_loads = [step(load_g, 4), both(step(load_g, 5), load_w)] + [step(load_weight, "wv", Wv, r) for r in range(4)]
+        later_loads = later_loads + [step(load_x, n) for n in range(6)]
+
+        def wo_half(half, loads):
+            for r in range(2):
+                for g in range(2):
+                    turn_weight("wo", 2 * half + r, g, turns[g])
+                loads[r]()
+
+        def quantize_wo(half):
+            return [step(quantize_weight, "wo", half, g) for g in range(2)]
+
+        wo_half(0, later_loads[0:2])
+        scene_0 = [step(turn_g, v, turns[v % 2]) for v in range(VIEWS)]
+        for r in range(3):
+            scene_0[2 * r + 1] = both(scene_0[2 * r + 1], later_loads[2 + r])
+        weave(scene_0, quantize_wo(0))
+        for n in range(CHUNKS):
+            quantize_g(n)
+        wo_half(1, later_loads[5:7])
+        for n in range(CHUNKS, 2 * CHUNKS):
+            quantize_g(n)
+        sort_g = [both(step(sort_words, ("g", r)), later_loads[4 + r]) for r in range(3, 6)]
+        weave(dmixed_jobs(0)[:3] + dmixed_jobs(1)[:3], quantize_wo(1) + sort_g + [sort_w])
+        scene_1 = [step(turn_g, v, turns[v % 2]) for v in range(VIEWS, 2 * VIEWS)]
+        for job in scene_1:
+            job()
+        turn_w(0, 4)
+        turn_w(4, 3)
+        sorts = [step(sort_words, ("wv", r)) for r in range(4)]
+        sorts[0] = both(sorts[0], later_loads[10])
+        sorts[1] = both(sorts[1], later_loads[11])
+        weave(
+            dmixed_jobs(0)[3:] + dmixed_jobs(1)[3:] + [step(dmixed, REST_TILE, half, act) for half in range(2)],
+            [step(quantize_g, REST_TILE), step(build_w_rest, 0), step(build_w_rest, 1)] + sorts[:3] + build_steps(0),
+        )
+        wv_jobs = [step(turn_weight, "wv", r, g, turns[g]) for r in range(4) for g in range(2)]
+        wv_jobs[1] = both(wv_jobs[1], sorts[3])
+        for half in range(2):
+            wv_jobs[4 * half + 3] = both(wv_jobs[4 * half + 3], step(quantize_weight, "wv", half, 0), step(quantize_weight, "wv", half, 1))
+        weave(
+            wv_jobs[:4] + [step(mix_rest, g, act) for g in range(2)] + mix_jobs(0)[:4] + wv_jobs[4:] + mix_jobs(0)[4:],
+            [step(quantize_g, n) for n in range(6, 12)] + build_steps(1),
+        )
+        weave(runs(dmixed_jobs(2), mix_jobs(1), 2, 3), fetch_steps(0) + build_steps(2) + x_steps(0) + feature_steps(0))
+        weave(
+            runs(dmixed_jobs(3), mix_jobs(2), 2, 3) + grad_x_jobs(0),
+            fetch_steps(1) + build_steps(3) + x_steps(2) + feature_steps(1),
+        )
+        first_turns = turn_dv_jobs(0, 0) + turn_dv_jobs(0, 1)
+        weave(
+            runs(mix_jobs(3), grad_x_jobs(1), 3, 2) + first_turns,
+            fetch_steps(2) + x_steps(4) + feature_steps(2),
+        )
+        weave(
+            turn_dv_jobs(1, 0, turns) + turn_dv_jobs(2, 0, turns),
+            [step(quantize_dv_tokens, 0, 0), step(quantize_dv_tokens, 0, 1), step(fetch, 3, 0), step(fetch, 3, 1)],
+        )
+        weave(
+            grad_x_jobs(2)[:2] + turn_dv_jobs(1, 1) + turn_dv_jobs(2, 1) + grad_x_jobs(2)[2:],
+            [step(quantize_dv_tokens, 1, 0), step(quantize_dv_tokens, 2, 0), step(weave_dv, 3, 0), step(weave_dv, 3, 1)],
+        )
+        weave(
+            [step(grad_w, 0, m, act) for m in range(8)],
+            [step(quantize_dv_tokens, 1, 1), step(quantize_dv_tokens, 2, 1), step(quantize_dv_features, 3, 0), step(quantize_dv_features, 3, 1)],
+        )
+        for job in grad_x_jobs(3, turns) + [step(grad_w, 1, m, turns[m % 2]) for m in range(8)]:
+            job()

@@ -95,10 +95,11 @@ def tile_crossviewattention_pa_v_kernel(tc, x, scores, Wv, bv, Wo, bo, w, grad_o
 
         def load_w():
             for b in range(SCENES):
-                nc.sync.dma_start(out=w_in[JH * b : JH * (b + 1)], in_=w[b].rearrange("i j h s -> (j h) i s"))
+                nc.scalar.dma_start(out=w_in[JH * b : JH * (b + 1)], in_=w[b].rearrange("i j h s -> (j h) i s"))
 
-        for r in range(2):
-            load_weight("wo", Wo, r)
+        load_weight("wo", Wo, 0)
+        load_w()
+        load_weight("wo", Wo, 1)
         for r in range(3):
             load_g(r)
         for r in range(2, 4):
@@ -209,6 +210,31 @@ def tile_crossviewattention_pa_v_kernel(tc, x, scores, Wv, bv, Wo, bo, w, grad_o
                     nc.tensor.transpose(slots[:, a, u, :], half_words((name, r), a, g, u), ident[:])
             dst = stage_words((name, half, g))[:, BANK * part : BANK * (part + 1)]
             copy(dst.rearrange("p (a c u) -> p a c u", a=2, u=2), slots.rearrange("p a u c -> p a c u"))
+
+        def load_wv(half, g):
+            t = tile("raw", [P, 16, P], BF16, bufs=8)
+            rows = Wv[BANK * half : BANK * (half + 1), :].rearrange("(n a) k -> a n k", a=32)
+            for q in range(4):
+                first = BANK * g + P * q
+                nc.sync.dma_start(out=t[32 * q : 32 * (q + 1)], in_=rows[:, :, first : first + P])
+            raw["wv", half, g] = t
+
+        turned = {}
+
+        def sort_wv(half, g):
+            ordered["wv", half, g] = tile("ordered", [P, 16, 2, 32], F32, bufs=3)
+            words = raw["wv", half, g][:].rearrange("p n k -> p (n k)").bitcast(F32)
+            act(ordered["wv", half, g][:], words.rearrange("p (n c u) -> p n u c", n=16, u=2))
+
+        def turn_wv(half, g):
+            turned[half, g] = tile("ordered", [P, 16, 2, 32], F32, bufs=3)
+            flat = "p n u c -> p (n u c)"
+            nc.vector.transpose(out=turned[half, g][:].rearrange(flat), in_=ordered["wv", half, g][:].rearrange(flat))
+
+        def pair_wv(half, g, copy):
+            new_stage(("wv", half, g))
+            dst = stage_words(("wv", half, g)).rearrange("p (n a u) -> p n a u", n=16, u=2)
+            copy(dst, turned[half, g][:].rearrange("p n u a -> p n a u"))
 
         def quantize_weight(name, half, g):
             cols = slice(BANK * half, BANK * (half + 1))
@@ -457,71 +483,79 @@ def tile_crossviewattention_pa_v_kernel(tc, x, scores, Wv, bv, Wo, bo, w, grad_o
         def x_steps(n):
             return [step(weave_x, n), step(weave_x, n + 1), step(quantize_x, n), step(quantize_x, n + 1)]
 
-        later_loads = [step(load_g, 4), both(step(load_g, 5), load_w)] + [step(load_weight, "wv", Wv, r) for r in range(4)]
+        later_loads = [step(load_g, 4), step(load_g, 5)] + [step(load_wv, half, g) for half in range(2) for g in range(2)]
         later_loads = later_loads + [step(load_x, n) for n in range(6)]
 
-        def wo_half(half, loads):
-            for r in range(2):
-                for g in range(2):
-                    turn_weight("wo", 2 * half + r, g, turns[g])
-                loads[r]()
+        def wo_rows(r, engines):
+            for g in range(2):
+                turn_weight("wo", r, g, engines[g])
 
-        def quantize_wo(half):
-            return [step(quantize_weight, "wo", half, g) for g in range(2)]
+        def quantize_half(name, half):
+            return [step(quantize_weight, name, half, g) for g in range(2)]
 
-        wo_half(0, later_loads[0:2])
-        scene_0 = [step(turn_g, v, turns[v % 2]) for v in range(VIEWS)]
-        for r in range(3):
-            scene_0[2 * r + 1] = both(scene_0[2 * r + 1], later_loads[2 + r])
-        weave(scene_0, quantize_wo(0))
-        for n in range(CHUNKS):
-            quantize_g(n)
-        wo_half(1, later_loads[5:7])
-        for n in range(CHUNKS, 2 * CHUNKS):
-            quantize_g(n)
-        sort_g = [both(step(sort_words, ("g", r)), later_loads[4 + r]) for r in range(3, 6)]
-        weave(dmixed_jobs(0)[:3] + dmixed_jobs(1)[:3], quantize_wo(1) + sort_g + [sort_w])
-        scene_1 = [step(turn_g, v, turns[v % 2]) for v in range(VIEWS, 2 * VIEWS)]
-        for job in scene_1:
-            job()
+        def wv_steps(half):
+            steps = [step(fn, half, g) for fn in (sort_wv, turn_wv) for g in range(2)]
+            steps = [steps[0], steps[2], steps[1], step(pair_wv, half, 0, dve), steps[3]]
+            return steps + [step(quantize_weight, "wv", half, 0), step(pair_wv, half, 1, dve)]
+
+        sort_w()
+        wo_rows(0, (act, act))
+        later_loads[0]()
         turn_w(0, 4)
         turn_w(4, 3)
-        sorts = [step(sort_words, ("wv", r)) for r in range(4)]
-        sorts[0] = both(sorts[0], later_loads[10])
-        sorts[1] = both(sorts[1], later_loads[11])
+        wo_rows(1, turns)
+        later_loads[1]()
+        scene_0 = [step(turn_g, v, act) for v in range(VIEWS - 1)] + [step(turn_g, VIEWS - 1, dve)]
+        for r in range(3):
+            scene_0[2 * r + 1] = both(scene_0[2 * r + 1], later_loads[2 + r])
+        weave(scene_0[:4], build_steps(0)[:2] + quantize_half("wo", 0) + build_steps(0)[2:])
+        scene_0[4]()
+        scene_0[5]()
+        wo_rows(2, (act, act))
+        later_loads[5]()
+        for n in range(CHUNKS):
+            quantize_g(n)
+        sort_words(("wo", 3))
+        later_loads[6]()
+        for job in dmixed_jobs(0, turns)[:3]:
+            job()
+        wo_rows(3, turns)
+        weave(mix_jobs(0)[:3] + [step(mix, 0, 3, act)], quantize_half("wo", 1) + [step(quantize_g, n) for n in range(CHUNKS, 2 * CHUNKS)])
+        sort_g = [both(step(sort_words, ("g", r)), later_loads[4 + r]) for r in range(3, 6)]
+        weave(dmixed_jobs(0)[3:] + dmixed_jobs(1)[:3], sort_g + build_steps(1)[:2])
+        for v in range(VIEWS, 2 * VIEWS):
+            turn_g(v, turns[v % 2])
+        weave(mix_jobs(0)[4:7] + [step(mix, 0, 7, act)], wv_steps(0)[:1] + [step(quantize_g, REST_TILE)] + build_steps(1)[2:] + [step(build_w_rest, 0), step(build_w_rest, 1)] + wv_steps(0)[1:5])
         weave(
-            dmixed_jobs(0)[3:] + dmixed_jobs(1)[3:] + [step(dmixed, REST_TILE, half, act) for half in range(2)],
-            [step(quantize_g, REST_TILE), step(build_w_rest, 0), step(build_w_rest, 1)] + sorts[:3] + build_steps(0),
+            dmixed_jobs(1)[3:] + [step(dmixed, REST_TILE, half, act) for half in range(2)],
+            [step(quantize_g, n) for n in range(6, 12)] + wv_steps(0)[5:] + later_loads[10:],
         )
-        wv_jobs = [step(turn_weight, "wv", r, g, turns[g]) for r in range(4) for g in range(2)]
-        wv_jobs[1] = both(wv_jobs[1], sorts[3])
-        for half in range(2):
-            wv_jobs[4 * half + 3] = both(wv_jobs[4 * half + 3], step(quantize_weight, "wv", half, 0), step(quantize_weight, "wv", half, 1))
+        rest_jobs = [both(step(mix_rest, g, act), step(park, 0, g)) for g in range(2)]
         weave(
-            wv_jobs[:4] + [step(mix_rest, g, act) for g in range(2)] + mix_jobs(0)[:4] + wv_jobs[4:] + mix_jobs(0)[4:],
-            [step(quantize_g, n) for n in range(6, 12)] + build_steps(1),
-        )
-        weave(runs(dmixed_jobs(2), mix_jobs(1), 2, 3), fetch_steps(0) + build_steps(2) + x_steps(0) + feature_steps(0))
-        weave(
-            runs(dmixed_jobs(3), mix_jobs(2), 2, 3) + grad_x_jobs(0),
-            fetch_steps(1) + build_steps(3) + x_steps(2) + feature_steps(1),
-        )
-        first_turns = turn_dv_jobs(0, 0) + turn_dv_jobs(0, 1)
-        weave(
-            runs(mix_jobs(3), grad_x_jobs(1), 3, 2) + first_turns,
-            fetch_steps(2) + x_steps(4) + feature_steps(2),
+            mix_jobs(1)[:2] + rest_jobs + mix_jobs(1)[2:],
+            [step(quantize_weight, "wv", 0, 1)] + build_steps(2) + wv_steps(1) + fetch_steps(0) + x_steps(0)[:2],
         )
         weave(
-            turn_dv_jobs(1, 0, turns) + turn_dv_jobs(2, 0, turns),
-            [step(quantize_dv_tokens, 0, 0), step(quantize_dv_tokens, 0, 1), step(fetch, 3, 0), step(fetch, 3, 1)],
+            dmixed_jobs(2) + mix_jobs(2),
+            [step(quantize_weight, "wv", 1, 1)] + x_steps(0)[2:] + feature_steps(0) + fetch_steps(1) + build_steps(3),
+        )
+        weave(
+            dmixed_jobs(3) + grad_x_jobs(0),
+            feature_steps(1) + fetch_steps(2) + x_steps(2),
+        )
+        weave(mix_jobs(3), feature_steps(2) + x_steps(4)[:2])
+        fetch(3, 0)
+        weave(grad_x_jobs(1)[:2], x_steps(4)[2:])
+        fetch(3, 1)
+        weave(
+            grad_x_jobs(1)[2:] + turn_dv_jobs(0, 0) + turn_dv_jobs(0, 1) + turn_dv_jobs(1, 0, turns) + turn_dv_jobs(2, 0, turns),
+            [step(weave_dv, 3, 0), step(quantize_dv_tokens, 0, 0), step(quantize_dv_features, 3, 0), step(quantize_dv_tokens, 0, 1)],
         )
         weave(
             grad_x_jobs(2)[:2] + turn_dv_jobs(1, 1) + turn_dv_jobs(2, 1) + grad_x_jobs(2)[2:],
-            [step(quantize_dv_tokens, 1, 0), step(quantize_dv_tokens, 2, 0), step(weave_dv, 3, 0), step(weave_dv, 3, 1)],
+            [step(quantize_dv_tokens, 1, 0), step(quantize_dv_tokens, 2, 0), step(weave_dv, 3, 1), step(quantize_dv_features, 3, 1)],
         )
-        weave(
-            [step(grad_w, 0, m, act) for m in range(8)],
-            [step(quantize_dv_tokens, 1, 1), step(quantize_dv_tokens, 2, 1), step(quantize_dv_features, 3, 0), step(quantize_dv_features, 3, 1)],
-        )
-        for job in grad_x_jobs(3, turns) + [step(grad_w, 1, m, turns[m % 2]) for m in range(8)]:
-            job()
+        weave(grad_x_jobs(3, turns), [step(quantize_dv_tokens, 1, 1), step(quantize_dv_tokens, 2, 1)])
+        for g in range(2):
+            for m in range(8):
+                grad_w(g, m, turns[m % 2])

@@ -95,10 +95,12 @@ def tile_crossviewattention_pa_v_kernel(tc, x, scores, Wv, bv, Wo, bo, w, grad_o
 
         def load_w():
             for b in range(SCENES):
-                nc.scalar.dma_start(out=w_in[JH * b : JH * (b + 1)], in_=w[b].rearrange("i j h s -> (j h) i s"))
+                rows = w[b].rearrange("i j h s -> (j h) i s")
+                for lo, hi in ((0, 32), (32, JH)):
+                    nc.sync.dma_start(out=w_in[JH * b + lo : JH * b + hi], in_=rows[lo:hi])
 
-        load_weight("wo", Wo, 0)
         load_w()
+        load_weight("wo", Wo, 0)
         load_weight("wo", Wo, 1)
         for r in range(3):
             load_g(r)
@@ -214,7 +216,7 @@ def tile_crossviewattention_pa_v_kernel(tc, x, scores, Wv, bv, Wo, bo, w, grad_o
         def load_wv(half, g):
             t = tile("raw", [P, 16, P], BF16, bufs=8)
             rows = Wv[BANK * half : BANK * (half + 1), :].rearrange("(n a) k -> a n k", a=32)
-            for q in range(4):
+            for q in (0, 2, 1, 3):
                 first = BANK * g + P * q
                 nc.sync.dma_start(out=t[32 * q : 32 * (q + 1)], in_=rows[:, :, first : first + P])
             raw["wv", half, g] = t
@@ -224,7 +226,7 @@ def tile_crossviewattention_pa_v_kernel(tc, x, scores, Wv, bv, Wo, bo, w, grad_o
         def sort_wv(half, g):
             ordered["wv", half, g] = tile("ordered", [P, 16, 2, 32], F32, bufs=3)
             words = raw["wv", half, g][:].rearrange("p n k -> p (n k)").bitcast(F32)
-            act(ordered["wv", half, g][:], words.rearrange("p (n c u) -> p n u c", n=16, u=2))
+            turns[1 - half](ordered["wv", half, g][:], words.rearrange("p (n c u) -> p n u c", n=16, u=2))
 
         def turn_wv(half, g):
             turned[half, g] = tile("ordered", [P, 16, 2, 32], F32, bufs=3)
@@ -499,18 +501,27 @@ def tile_crossviewattention_pa_v_kernel(tc, x, scores, Wv, bv, Wo, bo, w, grad_o
             return steps + [step(quantize_weight, "wv", half, 0), step(pair_wv, half, 1, dve)]
 
         sort_w()
-        wo_rows(0, (act, act))
-        later_loads[0]()
         turn_w(0, 4)
         turn_w(4, 3)
-        wo_rows(1, turns)
+        wo_rows(0, (act, act))
+        later_loads[0]()
+        for build in build_steps(0):
+            build()
+        wo_rows(1, (act, act))
         later_loads[1]()
-        scene_0 = [step(turn_g, v, act) for v in range(VIEWS - 1)] + [step(turn_g, VIEWS - 1, dve)]
-        for r in range(3):
-            scene_0[2 * r + 1] = both(scene_0[2 * r + 1], later_loads[2 + r])
-        weave(scene_0[:4], build_steps(0)[:2] + quantize_half("wo", 0) + build_steps(0)[2:])
-        scene_0[4]()
-        scene_0[5]()
+        build_w_rest(0)
+        build_w_rest(1)
+        turn_g(0, act)
+        turn_g(1, dve)
+        later_loads[2]()
+        for quantize_wo in quantize_half("wo", 0):
+            quantize_wo()
+        turn_g(2, act)
+        turn_g(3, act)
+        later_loads[3]()
+        turn_g(4, dve)
+        turn_g(5, act)
+        later_loads[4]()
         wo_rows(2, (act, act))
         later_loads[5]()
         for n in range(CHUNKS):
@@ -522,17 +533,17 @@ def tile_crossviewattention_pa_v_kernel(tc, x, scores, Wv, bv, Wo, bo, w, grad_o
         wo_rows(3, turns)
         weave(mix_jobs(0)[:3] + [step(mix, 0, 3, act)], quantize_half("wo", 1) + [step(quantize_g, n) for n in range(CHUNKS, 2 * CHUNKS)])
         sort_g = [both(step(sort_words, ("g", r)), later_loads[4 + r]) for r in range(3, 6)]
-        weave(dmixed_jobs(0)[3:] + dmixed_jobs(1)[:3], sort_g + build_steps(1)[:2])
+        weave(dmixed_jobs(0)[3:] + dmixed_jobs(1)[:3], sort_g + build_steps(1))
         for v in range(VIEWS, 2 * VIEWS):
             turn_g(v, turns[v % 2])
-        weave(mix_jobs(0)[4:7] + [step(mix, 0, 7, act)], wv_steps(0)[:1] + [step(quantize_g, REST_TILE)] + build_steps(1)[2:] + [step(build_w_rest, 0), step(build_w_rest, 1)] + wv_steps(0)[1:5])
+        weave(mix_jobs(0)[4:7] + [step(mix, 0, 7, act)], [step(quantize_g, REST_TILE)] + [step(quantize_g, n) for n in range(6, 12)] + wv_steps(0)[:1])
         weave(
             dmixed_jobs(1)[3:] + [step(dmixed, REST_TILE, half, act) for half in range(2)],
-            [step(quantize_g, n) for n in range(6, 12)] + wv_steps(0)[5:] + later_loads[10:],
+            wv_steps(0)[1:] + later_loads[10:],
         )
         rest_jobs = [both(step(mix_rest, g, act), step(park, 0, g)) for g in range(2)]
         weave(
-            mix_jobs(1)[:2] + rest_jobs + mix_jobs(1)[2:],
+            mix_jobs(1)[:3] + rest_jobs + mix_jobs(1)[3:],
             [step(quantize_weight, "wv", 0, 1)] + build_steps(2) + wv_steps(1) + fetch_steps(0) + x_steps(0)[:2],
         )
         weave(
@@ -544,18 +555,14 @@ def tile_crossviewattention_pa_v_kernel(tc, x, scores, Wv, bv, Wo, bo, w, grad_o
             feature_steps(1) + fetch_steps(2) + x_steps(2),
         )
         weave(mix_jobs(3), feature_steps(2) + x_steps(4)[:2])
-        fetch(3, 0)
-        weave(grad_x_jobs(1)[:2], x_steps(4)[2:])
-        fetch(3, 1)
-        weave(
-            grad_x_jobs(1)[2:] + turn_dv_jobs(0, 0) + turn_dv_jobs(0, 1) + turn_dv_jobs(1, 0, turns) + turn_dv_jobs(2, 0, turns),
-            [step(weave_dv, 3, 0), step(quantize_dv_tokens, 0, 0), step(quantize_dv_features, 3, 0), step(quantize_dv_tokens, 0, 1)],
-        )
-        weave(
-            grad_x_jobs(2)[:2] + turn_dv_jobs(1, 1) + turn_dv_jobs(2, 1) + grad_x_jobs(2)[2:],
-            [step(quantize_dv_tokens, 1, 0), step(quantize_dv_tokens, 2, 0), step(weave_dv, 3, 1), step(quantize_dv_features, 3, 1)],
-        )
-        weave(grad_x_jobs(3, turns), [step(quantize_dv_tokens, 1, 1), step(quantize_dv_tokens, 2, 1)])
+        weave(grad_x_jobs(1), x_steps(4)[2:] + fetch_steps(3))
         for g in range(2):
-            for m in range(8):
-                grad_w(g, m, turns[m % 2])
+            for gam in range(3):
+                for job in turn_dv_jobs(gam, g, turns):
+                    job()
+            if g == 0:
+                weave(grad_x_jobs(2), [step(quantize_dv_tokens, gam, 0) for gam in range(3)])
+        dw_jobs = [step(grad_w, g, m, turns[m % 2] if g else act) for g in range(2) for m in range(8)]
+        weave(dw_jobs[:8], feature_steps(3)[:1] + [step(quantize_dv_tokens, gam, 1) for gam in range(3)] + feature_steps(3)[1:])
+        for job in grad_x_jobs(3, turns) + dw_jobs[8:]:
+            job()

from contextlib import ExitStack

import concourse.mybir as mybir
from concourse.masks import make_identity

F32 = mybir.dt.float32
BF16 = mybir.dt.bfloat16
U32 = mybir.dt.uint32
U8 = mybir.dt.uint8
E4M3 = mybir.dt.float8_e4m3fn_x4
E5M2 = mybir.dt.float8_e5m2_x4
ALU = mybir.AluOpType
AXIS = mybir.AxisListType

SCENES, VIEWS, S, D, HEADS = 2, 6, 128, 1024, 8
TOKENS = SCENES * VIEWS * S
P = 128
BANK = 512
POS = 20
CHUNKS = 3
ROWS = VIEWS * POS
REST = 4
GROUP = CHUNKS * POS + REST
REST_TILE = 4 * CHUNKS
JH = VIEWS * HEADS
PARK_ROW = 256

FLOPS = 3 * 2 * TOKENS * D * D + 2 * VIEWS * TOKENS * D
BYTES = 2 * (2 * TOKENS * D + 2 * D * D) + 4 * SCENES * VIEWS * VIEWS * HEADS * S + 4 * (TOKENS * D + D * D)


def weave(jobs, side):
    done = 0
    for n, job in enumerate(jobs):
        job()
        upto = (n + 1) * len(side) // len(jobs)
        for step in side[done:upto]:
            step()
        done = upto


def runs(first, second, a, b):
    merged = []
    for n in range(max(-(-len(first) // a), -(-len(second) // b))):
        merged.extend(first[n * a : (n + 1) * a])
        merged.extend(second[n * b : (n + 1) * b])
    return merged


def tile_crossviewattention_pa_v_kernel(tc, x, scores, Wv, bv, Wo, bo, w, grad_out, out_0, out_1):
    nc = tc.nc
    with ExitStack() as ctx:
        sb = ctx.enter_context(tc.tile_pool(name="sb", bufs=1))
        psum = ctx.enter_context(tc.psum_pool(name="psum", bufs=8))
        ctx.enter_context(tc.manual_schedule())

        def tile(name, shape, dtype, tag=None, bufs=1):
            return sb.tile(shape, dtype, name=name, tag=tag or name, bufs=bufs, align_bytes=64)

        def bank():
            return psum.tile([P, BANK], F32, name="bank", tag="bank")

        def act(out, in_):
            nc.scalar.copy(out=out, in_=in_)

        def dve(out, in_):
            nc.vector.tensor_copy(out=out, in_=in_)

        def quantize(codes, scales, values, fmt):
            nc.vector.quantize_mx(out=codes.bitcast(fmt), scales=scales, in_=values)

        raw = {}

        def load_rows(key, src):
            t = tile("raw", [P, 2, D], BF16, bufs=8)
            nc.sync.dma_start(out=t[:], in_=src)
            raw[key] = t

        def load_weight(name, W, r):
            load_rows((name, r), W[2 * P * r : 2 * P * (r + 1), :].rearrange("(a p) k -> p a k", p=P))

        def load_g(r):
            load_rows(("g", r), grad_out[2 * r : 2 * r + 2].rearrange("v s k -> s v k"))

        x_rows = x.rearrange("v s d -> (v s) d")

        def load_x(n):
            gam, half = divmod(n, 2)
            t = tile("raw", [P, 4, BANK], BF16, bufs=8)
            src = x_rows[512 * gam : 512 * (gam + 1), BANK * half : BANK * (half + 1)]
            nc.sync.dma_start(out=t[:], in_=src.rearrange("(p j) d -> p j d", j=4))
            raw["x", n] = t

        w_in = tile("w_in", [P, VIEWS, S], F32, tag="back", bufs=2)

        def load_w():
            for b in range(SCENES):
                rows = w[b].rearrange("i j h s -> (j h) i s")
                for lo, hi in ((0, 32), (32, JH)):
                    nc.sync.dma_start(out=w_in[JH * b + lo : JH * b + hi], in_=rows[lo:hi])

        load_w()
        load_weight("wo", Wo, 0)
        load_weight("wo", Wo, 1)
        for r in range(3):
            load_g(r)
        for r in range(2, 4):
            load_weight("wo", Wo, r)
        load_g(3)

        ident = tile("ident", [P, P], F32)
        make_identity(nc, ident[:])
        w_sorted = tile("w_sorted", [P, 7, P], F32, tag="back", bufs=2)
        nc.vector.memset(w_sorted[:], 0.0)
        g_stage = [tile("g_stage", [P, 6, 2, P, 2], F32, tag="wide", bufs=2) for b in range(SCENES)]
        g_rest = tile("g_rest", [P, 2, P, 2], F32)
        for b in range(SCENES):
            nc.vector.memset(g_stage[b][:, :, :, ROWS:, :], 0.0)
        nc.vector.memset(g_rest[:, :, 2 * JH :, :], 0.0)
        perm = tile("perm", [P, P], F32)
        dve(perm[:, :ROWS].rearrange("r (u p e) -> r u p e", u=2, e=2), ident[:, :ROWS].rearrange("r (p u e) -> r u p e", u=2, e=2))
        dve(perm[:, ROWS:].rearrange("r (u p e) -> r u p e", u=2, e=2), ident[:, ROWS:].rearrange("r (p u e) -> r u p e", u=2, e=2))
        mask = tile("mask", [P, POS], F32)
        nc.vector.tensor_reduce(out=mask[:], in_=ident[:, :ROWS].rearrange("r (i s) -> r s i", i=VIEWS), axis=AXIS.X, op=ALU.add)
        mask_rest = tile("mask_rest", [P, SCENES, 8], F32)
        nc.vector.tensor_reduce(
            out=mask_rest[:], in_=ident[:, : 2 * JH].rearrange("r (b i s) -> r b s i", b=SCENES, i=VIEWS), axis=AXIS.X, op=ALU.add
        )

        used = 2 * JH

        def sort_w():
            for u in range(2):
                dve(
                    w_sorted[:used, CHUNKS * u : CHUNKS * (u + 1), :ROWS].rearrange("q k (i p e) -> q k i p e", i=VIEWS, e=2),
                    w_in[:used, :, :ROWS].rearrange("q i (k p u e) -> q u k i p e", k=CHUNKS, u=2, e=2)[:, u],
                )
            for b in range(SCENES):
                dve(
                    w_sorted[:used, 6, JH * b : JH * (b + 1)].rearrange("q (i u p e) -> q i u p e", i=VIEWS, u=2, e=2),
                    w_in[:used, :, ROWS:].rearrange("q i (p u e) -> q i u p e", u=2, e=2),
                )

        w_rows = tile("w_rows", [P, SCENES, 6, HEADS, VIEWS], F32)
        w_rows_rest = tile("w_rows_rest", [P, SCENES, HEADS, VIEWS], F32)

        def turn_w(first, count):
            acc = bank()
            slots = acc[:].rearrange("r (n c) -> r n c", c=P)
            for n in range(count):
                nc.tensor.transpose(slots[:, n, :], w_sorted[:, first + n, :], ident[:])
            main = min(count, 6 - first)
            act(
                w_rows[:, :, first : first + main].rearrange("r b n h j -> r n b h j"),
                slots[:, :main, :used].rearrange("r n (b j h) -> r n b h j", b=SCENES, j=VIEWS),
            )
            if main < count:
                act(w_rows_rest[:], slots[:, main, :used].rearrange("r (b j h) -> r b h j", b=SCENES, j=VIEWS))

        mix_w = {}

        def build_w(st, lo, hi):
            b, u = divmod(st, 2)
            if lo == 0:
                mix_w[st] = tile("mix_w", [P, POS, CHUNKS * JH], F32, bufs=2)
            src = w_rows[:, b, CHUNKS * u : CHUNKS * (u + 1)].rearrange("r k h j -> r (k h j)")
            for s in range(lo, hi):
                nc.vector.tensor_scalar(out=mix_w[st][:, s, :], in0=src, scalar1=mask[:, s : s + 1], scalar2=None, op0=ALU.mult)

        def build_steps(st):
            return [lambda lo=lo: build_w(st, lo, lo + 5) for lo in range(0, POS, 5)]

        mix_w_rest = tile("mix_w_rest", [P, SCENES, 8, JH], F32)

        def build_w_rest(b):
            src = w_rows_rest[:, b].rearrange("r h j -> r (h j)")
            for s in range(8):
                nc.vector.tensor_scalar(
                    out=mix_w_rest[:, b, s, :], in0=src, scalar1=mask_rest[:, b, s : s + 1], scalar2=None, op0=ALU.mult
                )

        w_codes = {name: tile(name + "_codes", [P, 2, D], U32) for name in ("wo", "wv")}
        w_scales = {name: tile(name + "_scales", [P, 2, D], U8) for name in ("wo", "wv")}
        stage = {}

        def new_stage(key, width=BANK):
            stage[key] = tile("stage", [P, width, 4], BF16, bufs=4)

        def stage_words(key):
            return stage[key][:].rearrange("p c t -> p (c t)").bitcast(F32)

        ordered = {}

        def sort_words(key):
            ordered[key] = tile("ordered", [P, 4, 2, P], F32, bufs=3)
            words = raw[key][:].rearrange("p a k -> p (a k)").bitcast(F32)
            dve(ordered[key][:], words.rearrange("p (n c u) -> p n u c", n=4, u=2))

        def half_words(key, a, g, u):
            if key in ordered:
                return ordered[key][:, 2 * a + g, u, :]
            return raw[key][:, a, :].bitcast(F32)[:, 256 * g + u : 256 * (g + 1) : 2]

        def turn_weight(name, r, g, copy):
            half, part = divmod(r, 2)
            if part == 0:
                new_stage((name, half, g))
            acc = bank()
            slots = acc[:].rearrange("p (a u c) -> p a u c", a=2, u=2)
            for a in range(2):
                for u in range(2):
                    nc.tensor.transpose(slots[:, a, u, :], half_words((name, r), a, g, u), ident[:])
            dst = stage_words((name, half, g))[:, BANK * part : BANK * (part + 1)]
            copy(dst.rearrange("p (a c u) -> p a c u", a=2, u=2), slots.rearrange("p a u c -> p a c u"))

        def load_wv(half, g):
            t = tile("raw", [P, 16, P], BF16, bufs=8)
            rows = Wv[BANK * half : BANK * (half + 1), :].rearrange("(n a) k -> a n k", a=32)
            for q in (0, 2, 1, 3):
                first = BANK * g + P * q
                nc.sync.dma_start(out=t[32 * q : 32 * (q + 1)], in_=rows[:, :, first : first + P])
            raw["wv", half, g] = t

        turned = {}

        def sort_wv(half, g):
            ordered["wv", half, g] = tile("ordered", [P, 16, 2, 32], F32, bufs=3)
            words = raw["wv", half, g][:].rearrange("p n k -> p (n k)").bitcast(F32)
            turns[1 - half](ordered["wv", half, g][:], words.rearrange("p (n c u) -> p n u c", n=16, u=2))

        def turn_wv(half, g):
            turned[half, g] = tile("ordered", [P, 16, 2, 32], F32, bufs=3)
            flat = "p n u c -> p (n u c)"
            nc.vector.transpose(out=turned[half, g][:].rearrange(flat), in_=ordered["wv", half, g][:].rearrange(flat))

        def pair_wv(half, g, copy):
            new_stage(("wv", half, g))
            dst = stage_words(("wv", half, g)).rearrange("p (n a u) -> p n a u", n=16, u=2)
            copy(dst, turned[half, g][:].rearrange("p n u a -> p n a u"))

        def quantize_weight(name, half, g):
            cols = slice(BANK * half, BANK * (half + 1))
            values = stage[name, half, g][:].rearrange("p c t -> p (c t)")
            quantize(w_codes[name][:, g, cols], w_scales[name][:, g, cols], values, E4M3)

        g_codes = tile("g_codes", [P, REST_TILE + 1, 2 * P], U32, tag="codes")
        g_scales = tile("g_scales", [P, REST_TILE + 1, 2 * P], U8, tag="scales")

        def turn_g(v, copy):
            b, i = divmod(v, VIEWS)
            acc = bank()
            slots = acc[:].rearrange("p (g u n) -> p g u n", g=2, u=2)
            for g in range(2):
                for u in range(2):
                    nc.tensor.transpose(slots[:, g, u, :], half_words(("g", v // 2), v % 2, g, u), perm[:])
            copy(
                g_stage[b][:, :, :, POS * i : POS * (i + 1), :].rearrange("p k g s u -> p g k s u"),
                slots[:, :, :, :ROWS].rearrange("p g u (k s) -> p g k s u", s=POS),
            )
            col = JH * b + 8 * i
            copy(g_rest[:, :, col : col + 8, :], slots[:, :, :, ROWS:].rearrange("p g u s -> p g s u"))

        def quantize_g(n):
            src = g_rest[:] if n == REST_TILE else g_stage[n // 6][:, n % 6]
            values = src.rearrange("p g c u -> p (g c u)").bitcast(BF16)
            quantize(g_codes[:, n, :], g_scales[:, n, :], values, E5M2)

        dm = {}

        def dmixed(n, half, copy):
            if half == 0:
                if n == REST_TILE:
                    dm[n] = tile("dm_rest", [P, D], F32)
                else:
                    dm[n] = tile("dm", [P, D], F32, bufs=6)
            cols = slice(BANK * half, BANK * (half + 1))
            acc = bank()
            for g in range(2):
                rows = slice(P * g, P * (g + 1))
                nc.tensor.matmul_mx(
                    out=acc[:],
                    lhsT=g_codes[:, n, rows].bitcast(E5M2),
                    lhsT_scale=g_scales[:, n, rows],
                    rhs=w_codes["wo"][:, g, cols].bitcast(E4M3),
                    rhs_scale=w_scales["wo"][:, g, cols],
                    start=(g == 0),
                    stop=(g == 1),
                )
            copy(dm[n][:, cols], acc[:])

        dv_t = {(u, g): tile("dv_t%d%d" % (u, g), [P, 4, SCENES * VIEWS, GROUP], BF16) for u in range(2) for g in range(2)}

        def mix(st, h, copy):
            b, u = divmod(st, 2)
            acc = bank()
            for k in range(CHUNKS):
                col = JH * k + VIEWS * h
                nc.tensor.matmul(
                    out=acc[:, ROWS * k : ROWS * (k + 1)].rearrange("c (s j) -> c s j", j=VIEWS),
                    lhsT=dm[CHUNKS * st + k][:, P * h : P * (h + 1)],
                    rhs=mix_w[st][:, :, col : col + VIEWS],
                    start=True,
                    stop=True,
                )
            copy(
                dv_t[u, h // 4][:, h % 4, VIEWS * b : VIEWS * (b + 1), : CHUNKS * POS],
                acc[:, : CHUNKS * ROWS].rearrange("c (q j) -> c j q", j=VIEWS),
            )

        def mix_rest(g, copy):
            acc = bank()
            for hq in range(4):
                h = 4 * g + hq
                nc.tensor.matmul(
                    out=acc[:, used * hq : used * (hq + 1)].rearrange("c (s j) -> c s j", j=VIEWS),
                    lhsT=dm[REST_TILE][:, P * h : P * (h + 1)],
                    rhs=mix_w_rest[:].rearrange("r b s m -> r (b s) m")[:, :, VIEWS * h : VIEWS * (h + 1)],
                    start=True,
                    stop=True,
                )
            src = acc[:, : 4 * used].rearrange("c (h b u q j) -> c u h b j q", h=4, b=SCENES, u=2, j=VIEWS)
            for u in range(2):
                dst = dv_t[u, g][:, :, :, CHUNKS * POS :].rearrange("c h (b j) q -> c h b j q", b=SCENES)
                copy(dst, src[:, u])

        width = VIEWS * GROUP
        back = {}
        f_codes, f_scales = {}, {}

        def parking(st, g):
            rows = out_1[PARK_ROW + 192 * st : PARK_ROW + 192 * (st + 1), :]
            return rows.bitcast(BF16).rearrange("a b -> (a b)").rearrange("(c m) -> c m", m=width)[BANK * g : BANK * (g + 1), :]

        def park(st, g):
            b, u = divmod(st, 2)
            src = dv_t[u, g][:, :, VIEWS * b : VIEWS * (b + 1), :].rearrange("c h v q -> c h (v q)")
            nc.sync.dma_start(out=parking(st, g).rearrange("(h c) m -> c h m", c=P), in_=src)

        def fetch(st, g):
            back[st, g] = tile("back", [P, 4, width], BF16, tag="back", bufs=2)
            nc.sync.dma_start(out=back[st, g][:], in_=parking(st, g).rearrange("(p t) m -> p t m", t=4))

        def interleave(key, src):
            dve(stage[key][:].rearrange("p (c i) t -> p c t i", i=4), src.rearrange("p t (c i) -> p c t i", i=4))

        def weave_dv(st, g):
            new_stage(("f", st, g), width)
            interleave(("f", st, g), back[st, g][:])

        def quantize_dv_features(st, g):
            if g == 0:
                f_codes[st] = tile("f_codes", [P, 2, width], U32, bufs=2)
                f_scales[st] = tile("f_scales", [P, 2, width], U8, bufs=2)
            values = stage["f", st, g][:].rearrange("p c t -> p (c t)")
            for lo, hi in ((0, 256), (256, width)):
                quantize(f_codes[st][:, g, lo:hi], f_scales[st][:, g, lo:hi], values[:, 4 * lo : 4 * hi], E5M2)

        x_codes = tile("x_codes", [P, 3, D], U32)
        x_scales = tile("x_scales", [P, 3, D], U8)

        def weave_x(n):
            new_stage(("x", n))
            interleave(("x", n), raw["x", n][:])

        def quantize_x(n):
            gam, half = divmod(n, 2)
            cols = slice(BANK * half, BANK * (half + 1))
            quantize(x_codes[:, gam, cols], x_scales[:, gam, cols], stage["x", n][:].rearrange("p c t -> p (c t)"), E4M3)

        t_planes = {}

        def turn_dv(gam, g, part, copy):
            if part == 0:
                new_stage(("t", gam, g))
            acc = bank()
            slots = acc[:].rearrange("p (a u c) -> p a u c", a=2, u=2)
            for a in range(2):
                for u in range(2):
                    words = dv_t[u, g][:, 2 * part + a].rearrange("c v q -> c (v q)").bitcast(F32)
                    nc.tensor.transpose(slots[:, a, u, :], words[:, P * gam : P * (gam + 1)], ident[:])
            dst = stage_words(("t", gam, g))[:, BANK * part : BANK * (part + 1)]
            copy(dst.rearrange("p (a c u) -> p a c u", a=2, u=2), slots.rearrange("p a u c -> p a c u"))

        def quantize_dv_tokens(gam, g):
            if not t_planes:
                t_planes["codes"] = tile("t_codes", [P, 3, D], U32, tag="codes")
                t_planes["scales"] = tile("t_scales", [P, 3, D], U8, tag="scales")
            cols = slice(BANK * g, BANK * (g + 1))
            values = stage["t", gam, g][:].rearrange("p c t -> p (c t)")
            quantize(t_planes["codes"][:, gam, cols], t_planes["scales"][:, gam, cols], values, E5M2)

        ring = []
        taken = []

        def out_slot():
            if not ring:
                for n in range(2):
                    t = tile("ring", [P, 3, D], F32, tag="wide", bufs=2)
                    ring.extend(t[:, k, :] for k in range(3))
            taken.append(ring[len(taken) % len(ring)])
            return taken[-1]

        dx_rows = out_0.rearrange("v (p u e) d -> u e (v p) d", u=2, e=2)
        held = {}

        def grad_x(st, m, half, copy):
            b, u = divmod(st, 2)
            if half == 0:
                held[st, m] = out_slot()
            cols = slice(BANK * half, BANK * (half + 1))
            rows = slice(P * m, P * (m + 1))
            acc = bank()
            for g in range(2):
                nc.tensor.matmul_mx(
                    out=acc[:],
                    lhsT=f_codes[st][:, g, rows].bitcast(E5M2),
                    lhsT_scale=f_scales[st][:, g, rows],
                    rhs=w_codes["wv"][:, g, cols].bitcast(E4M3),
                    rhs_scale=w_scales["wv"][:, g, cols],
                    start=(g == 0),
                    stop=(g == 1),
                )
            copy(held[st, m][:, cols], acc[:])
            if half == 1:
                first = 32 * (VIEWS * b + 2 * m)
                for e in range(2):
                    nc.sync.dma_start(out=dx_rows[u, e, first : first + 64, :], in_=held[st, m][e::2, :])

        def grad_w(g, m, copy):
            if m % 2 == 0:
                held[g, "w", m // 2] = out_slot()
            dst = held[g, "w", m // 2][:, BANK * (m % 2) : BANK * (m % 2 + 1)]
            cols = slice(BANK * g, BANK * (g + 1))
            rows = slice(P * m, P * (m + 1))
            acc = bank()
            for gam in range(3):
                nc.tensor.matmul_mx(
                    out=acc[:],
                    lhsT=x_codes[:, gam, rows].bitcast(E4M3),
                    lhsT_scale=x_scales[:, gam, rows],
                    rhs=t_planes["codes"][:, gam, cols].bitcast(E5M2),
                    rhs_scale=t_planes["scales"][:, gam, cols],
                    start=(gam == 0),
                    stop=(gam == 2),
                )
            copy(dst, acc[:])
            nc.sync.dma_start(out=out_1[rows, cols], in_=dst)

        def step(fn, *args):
            return lambda: fn(*args)

        def both(*steps):
            return lambda: [s() for s in steps]

        turns = (act, dve)

        def dmixed_jobs(st, engines=(act,)):
            tiles = [(CHUNKS * st + k, half) for half in range(2) for k in range(CHUNKS)]
            return [step(dmixed, n, half, engines[c % len(engines)]) for c, (n, half) in enumerate(tiles)]

        def mix_jobs(st, engines=(act,)):
            jobs = [step(mix, st, h, engines[h % len(engines)]) for h in range(HEADS)]
            for g in range(2):
                jobs[4 * g + 3] = both(jobs[4 * g + 3], step(park, st, g))
            return jobs

        def grad_x_jobs(st, engines=(act,)):
            tiles = [(m, half) for m in range(3) for half in range(2)]
            return [step(grad_x, st, m, half, engines[c % len(engines)]) for c, (m, half) in enumerate(tiles)]

        def turn_dv_jobs(gam, g, engines=(act,)):
            return [step(turn_dv, gam, g, part, engines[part % len(engines)]) for part in range(2)]

        def feature_steps(st):
            return [
                step(weave_dv, st, 0),
                step(weave_dv, st, 1),
                step(quantize_dv_features, st, 0),
                step(quantize_dv_features, st, 1),
            ]

        def fetch_steps(st):
            return [step(fetch, st, 0), step(fetch, st, 1)]

        def x_steps(n):
            return [step(weave_x, n), step(weave_x, n + 1), step(quantize_x, n), step(quantize_x, n + 1)]

        later_loads = [step(load_g, 4), step(load_g, 5)] + [step(load_wv, half, g) for half in range(2) for g in range(2)]
        later_loads = later_loads + [step(load_x, n) for n in range(6)]

        def wo_rows(r, engines):
            for g in range(2):
                turn_weight("wo", r, g, engines[g])

        def quantize_half(name, half):
            return [step(quantize_weight, name, half, g) for g in range(2)]

        def wv_steps(half):
            steps = [step(fn, half, g) for fn in (sort_wv, turn_wv) for g in range(2)]
            steps = [steps[0], steps[2], steps[1], step(pair_wv, half, 0, dve), steps[3]]
            return steps + [step(quantize_weight, "wv", half, 0), step(pair_wv, half, 1, dve)]

        sort_w()
        turn_w(0, 4)
        turn_w(4, 3)
        wo_rows(0, (act, act))
        later_loads[0]()
        for build in build_steps(0):
            build()
        wo_rows(1, (act, act))
        later_loads[1]()
        build_w_rest(0)
        build_w_rest(1)
        turn_g(0, act)
        turn_g(1, dve)
        later_loads[2]()
        for quantize_wo in quantize_half("wo", 0):
            quantize_wo()
        turn_g(2, act)
        turn_g(3, act)
        later_loads[3]()
        turn_g(4, dve)
        turn_g(5, act)
        later_loads[4]()
        wo_rows(2, (act, act))
        later_loads[5]()
        for n in range(CHUNKS):
            quantize_g(n)
        sort_words(("wo", 3))
        later_loads[6]()
        for job in dmixed_jobs(0, turns)[:3]:
            job()
        wo_rows(3, turns)
        weave(mix_jobs(0)[:3] + [step(mix, 0, 3, act)], quantize_half("wo", 1) + [step(quantize_g, n) for n in range(CHUNKS, 2 * CHUNKS)])
        sort_g = [both(step(sort_words, ("g", r)), later_loads[4 + r]) for r in range(3, 6)]
        weave(dmixed_jobs(0)[3:] + dmixed_jobs(1)[:3], sort_g + build_steps(1))
        for v in range(VIEWS, 2 * VIEWS):
            turn_g(v, turns[v % 2])
        weave(mix_jobs(0)[4:7] + [step(mix, 0, 7, act)], [step(quantize_g, REST_TILE)] + [step(quantize_g, n) for n in range(6, 12)] + wv_steps(0)[:1])
        weave(
            dmixed_jobs(1)[3:] + [step(dmixed, REST_TILE, half, act) for half in range(2)],
            wv_steps(0)[1:] + later_loads[10:],
        )
        rest_jobs = [both(step(mix_rest, g, act), step(park, 0, g)) for g in range(2)]
        weave(
            mix_jobs(1)[:3] + rest_jobs + mix_jobs(1)[3:],
            [step(quantize_weight, "wv", 0, 1)] + build_steps(2) + wv_steps(1) + fetch_steps(0) + x_steps(0)[:2],
        )
        weave(
            dmixed_jobs(2) + mix_jobs(2),
            [step(quantize_weight, "wv", 1, 1)] + x_steps(0)[2:] + feature_steps(0) + fetch_steps(1) + build_steps(3),
        )
        weave(
            dmixed_jobs(3) + grad_x_jobs(0),
            feature_steps(1) + fetch_steps(2) + x_steps(2),
        )
        weave(mix_jobs(3), feature_steps(2) + x_steps(4)[:2])
        weave(grad_x_jobs(1), x_steps(4)[2:] + fetch_steps(3))
        for g in range(2):
            for gam in range(3):
                for job in turn_dv_jobs(gam, g, turns):
                    job()
            if g == 0:
                weave(grad_x_jobs(2), [step(quantize_dv_tokens, gam, 0) for gam in range(3)])
        dw_jobs = [step(grad_w, g, m, turns[m % 2] if g else act) for g in range(2) for m in range(8)]
        weave(dw_jobs[:8], feature_steps(3)[:1] + [step(quantize_dv_tokens, gam, 1) for gam in range(3)] + feature_steps(3)[1:])
        for job in grad_x_jobs(3, turns) + dw_jobs[8:]:
            job()
